import numpy as np
import ml_dtypes


def mxq(x, axis, fmt="e4m3"):
    dtype, down = {"e4m3": (ml_dtypes.float8_e4m3fn, 7), "e5m2": (ml_dtypes.float8_e5m2, 14)}[fmt]
    v = np.moveaxis(np.asarray(x, np.float32).astype(ml_dtypes.bfloat16).astype(np.float64), axis, -1)
    blocks = v.reshape(v.shape[:-1] + (-1, 32))
    amax = np.abs(blocks).max(-1, keepdims=True)
    byte = np.maximum(np.where(amax > 0, np.frexp(amax)[1] - 1 + 127, 0) - down, 1)
    scale = np.exp2(byte - 127.0)
    codes = (blocks / scale).astype(np.float32).astype(dtype).astype(np.float64)
    return np.moveaxis((codes * scale).reshape(v.shape), -1, axis)


WIDE = False


def mx_kscale(k):
    if not WIDE:
        return np.ones(k)
    levels = np.array([10, -10, 5, -5, 0])
    a = np.random.permutation(np.resize(levels, k // 512 * 4)).reshape(k // 512, 4)
    idx = np.arange(k)
    return np.exp2(a[idx // 512, idx % 128 // 32])


BF16 = ml_dtypes.bfloat16


def bf(x):
    return np.asarray(x, np.float32).astype(BF16)


def f64(x):
    return np.asarray(x).astype(np.float64)


N, B, T, C, R, O, NC, H, W = 4, 3072, 4, 128, 4, 512, 512, 16, 4
K = C * R
LEAKY_SLOPE = 0.01


def setup_inputs():
    s = mx_kscale(K)
    return {"pooled": bf((0.65 + 0.3 * np.random.standard_normal((N, B, K))) * s),
            "p": bf(0.65 + 0.5 * np.random.standard_normal((N, B, T, C))),
            "Wout": bf((4.0 / np.sqrt(K) * np.random.standard_normal((N, K, C)) - 4.0 / K) / s[None, :, None])}


def reference(pooled, p, Wout):
    y = mxq(f64(pooled), 2, "e4m3") @ mxq(f64(Wout), 1, "e4m3")
    y = np.where(y >= 0, y, LEAKY_SLOPE * y)
    return np.max(f64(p) + y[:, :, None, :], axis=2)

@@ -1,0 +1,158 @@
+from contextlib import ExitStack
+
+import concourse.mybir as mybir
+from concourse.masks import make_identity
+
+F32 = mybir.dt.float32
+BF16 = mybir.dt.bfloat16
+U32 = mybir.dt.uint32
+U8 = mybir.dt.uint8
+FP8X4 = mybir.dt.float8_e4m3fn_x4
+MAX = mybir.AluOpType.max
+ADD = mybir.AluOpType.add
+
+P = 128
+BINS = 4
+SAMPLES = 3072
+FRAMES = 4
+C = 128
+K = 512
+PACK = 4
+LEAKY_SLOPE = 0.01
+
+BLOCKS_PER_BIN = SAMPLES // P
+BLOCKS = 8
+CHUNKS_PER_BIN = BLOCKS_PER_BIN // BLOCKS
+CHUNKS = BINS * CHUNKS_PER_BIN
+WORDS = K // 2
+BANK = 512
+BLOCKS_PER_Y_BANK = BANK // C
+LEAD = 1
+
+FLOPS = 2 * BINS * SAMPLES * K * C
+
+
+def tile_gmpahead_pa_t_kernel(tc, pooled, p, Wout, out):
+    nc = tc.nc
+
+    pooled_rows = pooled.rearrange("n (q r) k -> n q (r k)", q=P)
+    frames_rows = p.rearrange("n (q r) t c -> n q (r t c)", q=P)
+    out_rows = out.rearrange("n (q r) c -> n q (r c)", q=P)
+
+    with ExitStack() as ctx:
+        const = ctx.enter_context(tc.tile_pool(name="const", bufs=1))
+        x_pool = ctx.enter_context(tc.tile_pool(name="x", bufs=4))
+        frames_pool = ctx.enter_context(tc.tile_pool(name="frames", bufs=4))
+        mx_pool = ctx.enter_context(tc.tile_pool(name="mx", bufs=2))
+        work = ctx.enter_context(tc.tile_pool(name="work", bufs=2))
+        leaky_pool = ctx.enter_context(tc.tile_pool(name="leaky", bufs=LEAD + 2))
+        feat_pool = ctx.enter_context(tc.tile_pool(name="feat", bufs=4))
+        xt_pool = ctx.enter_context(tc.psum_pool(name="xt", bufs=4))
+        y_pool = ctx.enter_context(tc.psum_pool(name="y", bufs=4))
+
+        ident = const.tile([P, P], F32)
+        make_identity(nc, ident[:])
+
+        def chunk_place(i):
+            return i // CHUNKS_PER_BIN, (i % CHUNKS_PER_BIN) * BLOCKS
+
+        def load_pooled(i):
+            n, r0 = chunk_place(i)
+            x_sb = x_pool.tile([P, BLOCKS * K], BF16)
+            nc.sync.dma_start(out=x_sb[:], in_=pooled_rows[n, :, r0 * K : (r0 + BLOCKS) * K])
+            return x_sb
+
+        def quantise_weights():
+            w_raw = const.tile([P, BINS * PACK * C], BF16)
+            nc.sync.dma_start(
+                out=w_raw[:].rearrange("q (g f) -> q g f", f=2 * C),
+                in_=Wout.rearrange("n k c -> (n k) c").rearrange("(g q e) c -> q g (e c)", q=P, e=2),
+            )
+            w_grouped = const.tile([P, BINS * C * PACK], BF16, align_bytes=64)
+            nc.vector.tensor_copy(
+                out=w_grouped[:].rearrange("q (n c t) -> q n c t", n=BINS, t=PACK),
+                in_=w_raw[:].rearrange("q (n t c) -> q n c t", n=BINS, t=PACK),
+            )
+            w_codes = const.tile([P, BINS * C], U32, align_bytes=64)
+            w_scales = const.tile([P, BINS * C], U8, align_bytes=64)
+            nc.vector.quantize_mx(out=w_codes[:].bitcast(FP8X4), scales=w_scales[:], in_=w_grouped[:])
+            return w_codes, w_scales
+
+        def quantise_pooled(x_sb):
+            x_words = x_sb[:].bitcast(F32)
+            grouped = mx_pool.tile([P, BLOCKS * P * PACK], BF16, align_bytes=64)
+            grouped_words = grouped[:].bitcast(F32)
+            for pair in range(BLOCKS // 2):
+                xt = xt_pool.tile([P, 2, 2, P], F32)
+                for blk in range(2):
+                    for u in range(2):
+                        first = ((2 * pair + blk) * 2 + u) * P
+                        nc.tensor.transpose(xt[:, blk, u, :], x_words[:, first : first + P], ident[:])
+                nc.scalar.copy(
+                    out=grouped_words[:, pair * BANK : (pair + 1) * BANK].rearrange(
+                        "q (k b u) -> q k b u", k=2, u=2
+                    ),
+                    in_=xt[:].rearrange("q k u b -> q k b u"),
+                )
+            codes = mx_pool.tile([P, BLOCKS * P], U32, align_bytes=64)
+            scales = mx_pool.tile([P, BLOCKS * P], U8, align_bytes=64)
+            nc.vector.quantize_mx(out=codes[:].bitcast(FP8X4), scales=scales[:], in_=grouped[:])
+            return codes, scales
+
+        def multiply_and_leaky(i, codes, scales):
+            n = chunk_place(i)[0]
+            w_cols = slice(n * C, (n + 1) * C)
+            slope_y = work.tile([P, BLOCKS * C], F32)
+            leaky = leaky_pool.tile([P, BLOCKS * C], F32)
+            for bank in range(BLOCKS // BLOCKS_PER_Y_BANK):
+                y_ps = y_pool.tile([P, BANK], F32)
+                for j in range(BLOCKS_PER_Y_BANK):
+                    b_cols = slice((bank * BLOCKS_PER_Y_BANK + j) * P, (bank * BLOCKS_PER_Y_BANK + j + 1) * P)
+                    nc.tensor.matmul_mx(
+                        out=y_ps[:, j * C : (j + 1) * C],
+                        lhsT=codes[:, b_cols].bitcast(FP8X4),
+                        lhsT_scale=scales[:, b_cols],
+                        rhs=w_codes[:, w_cols].bitcast(FP8X4),
+                        rhs_scale=w_scales[:, w_cols],
+                        start=True,
+                        stop=True,
+                    )
+                cols = slice(bank * BANK, (bank + 1) * BANK)
+                nc.scalar.mul(out=slope_y[:, cols], in_=y_ps[:], mul=LEAKY_SLOPE)
+                nc.vector.tensor_tensor(out=leaky[:, cols], in0=y_ps[:], in1=slope_y[:, cols], op=MAX)
+            return leaky
+
+        def add_frames_and_store(i, leaky):
+            n, r0 = chunk_place(i)
+            frames = frames_pool.tile([P, BLOCKS, FRAMES * C], BF16)
+            nc.sync.dma_start(
+                out=frames[:],
+                in_=frames_rows[n, :, r0 * FRAMES * C : (r0 + BLOCKS) * FRAMES * C].rearrange(
+                    "q (r f) -> q r f", f=FRAMES * C
+                ),
+            )
+            pair_max = work.tile([P, BLOCKS, 2 * C], BF16)
+            nc.vector.tensor_tensor(
+                out=pair_max[:], in0=frames[:, :, 0 : 2 * C], in1=frames[:, :, 2 * C : 4 * C], op=MAX
+            )
+            frame_max = work.tile([P, BLOCKS, C], BF16)
+            nc.vector.tensor_tensor(
+                out=frame_max[:], in0=pair_max[:, :, 0:C], in1=pair_max[:, :, C : 2 * C], op=MAX
+            )
+            feat = feat_pool.tile([P, BLOCKS * C], F32)
+            nc.vector.tensor_tensor(
+                out=feat[:], in0=leaky[:], in1=frame_max[:].rearrange("q r c -> q (r c)"), op=ADD
+            )
+            nc.sync.dma_start(out=out_rows[n, :, r0 * C : (r0 + BLOCKS) * C], in_=feat[:])
+
+        x_first = load_pooled(0)
+        w_codes, w_scales = quantise_weights()
+
+        leaky_of = {}
+        for step in range(CHUNKS + LEAD):
+            if step < CHUNKS:
+                x_sb = x_first if step == 0 else load_pooled(step)
+                codes, scales = quantise_pooled(x_sb)
+                leaky_of[step] = multiply_and_leaky(step, codes, scales)
+            if step >= LEAD:
+                add_frames_and_store(step - LEAD, leaky_of[step - LEAD])

@@ -20,14 +20,15 @@ K = 512
 PACK = 4
 LEAKY_SLOPE = 0.01
 
-BLOCKS_PER_BIN = SAMPLES // P
-BLOCKS = 8
-CHUNKS_PER_BIN = BLOCKS_PER_BIN // BLOCKS
+GROUPS = 8
+CHUNKS_PER_BIN = SAMPLES // (P * GROUPS)
 CHUNKS = BINS * CHUNKS_PER_BIN
-WORDS = K // 2
 BANK = 512
-BLOCKS_PER_Y_BANK = BANK // C
-LEAD = 1
+XT_BANKS = GROUPS * K // 2 // BANK
+Y_BANKS = GROUPS * C // BANK
+
+FRAME_LAG = 1
+AHEAD = 3
 
 FLOPS = 2 * BINS * SAMPLES * K * C
 
@@ -39,120 +40,158 @@ def tile_gmpahead_pa_t_kernel(tc, pooled, p, Wout, out):
     frames_rows = p.rearrange("n (q r) t c -> n q (r t c)", q=P)
     out_rows = out.rearrange("n (q r) c -> n q (r c)", q=P)
 
+    def dram_chunk(rows, j, width):
+        first = (j % CHUNKS_PER_BIN) * GROUPS * width
+        return rows[j // CHUNKS_PER_BIN, :, first : first + GROUPS * width]
+
     with ExitStack() as ctx:
         const = ctx.enter_context(tc.tile_pool(name="const", bufs=1))
-        x_pool = ctx.enter_context(tc.tile_pool(name="x", bufs=4))
-        frames_pool = ctx.enter_context(tc.tile_pool(name="frames", bufs=4))
-        mx_pool = ctx.enter_context(tc.tile_pool(name="mx", bufs=2))
+        x_pool = ctx.enter_context(tc.tile_pool(name="x", bufs=AHEAD + 2))
+        frames_pool = ctx.enter_context(tc.tile_pool(name="frames", bufs=AHEAD + 2))
         work = ctx.enter_context(tc.tile_pool(name="work", bufs=2))
-        leaky_pool = ctx.enter_context(tc.tile_pool(name="leaky", bufs=LEAD + 2))
+        leaky_pool = ctx.enter_context(tc.tile_pool(name="leaky", bufs=FRAME_LAG + 2))
         feat_pool = ctx.enter_context(tc.tile_pool(name="feat", bufs=4))
-        xt_pool = ctx.enter_context(tc.psum_pool(name="xt", bufs=4))
-        y_pool = ctx.enter_context(tc.psum_pool(name="y", bufs=4))
+        xt_pool = ctx.enter_context(tc.psum_pool(name="xt", bufs=XT_BANKS))
+        y_pool = ctx.enter_context(tc.psum_pool(name="y", bufs=2 * Y_BANKS))
 
         ident = const.tile([P, P], F32)
         make_identity(nc, ident[:])
+        w_raw = const.tile([P, BINS * PACK * C], BF16)
+        w_grouped = const.tile([P, BINS * C * PACK], BF16, align_bytes=64)
+        w_codes = const.tile([P, BINS * C], U32, align_bytes=64)
+        w_scales = const.tile([P, BINS * C], U8, align_bytes=64)
 
-        def chunk_place(i):
-            return i // CHUNKS_PER_BIN, (i % CHUNKS_PER_BIN) * BLOCKS
+        x_of, xt_of, grouped_of, codes_of, scales_of, y_of, slope_of, leaky_of = {}, {}, {}, {}, {}, {}, {}, {}
+        frames_of, pair_of, fmax_of = {}, {}, {}
 
-        def load_pooled(i):
-            n, r0 = chunk_place(i)
-            x_sb = x_pool.tile([P, BLOCKS * K], BF16)
-            nc.sync.dma_start(out=x_sb[:], in_=pooled_rows[n, :, r0 * K : (r0 + BLOCKS) * K])
-            return x_sb
+        def load_pooled(j):
+            x_sb = x_pool.tile([P, GROUPS * K], BF16)
+            nc.sync.dma_start(out=x_sb[:], in_=dram_chunk(pooled_rows, j, K))
+            x_of[j] = x_sb
 
-        def quantise_weights():
-            w_raw = const.tile([P, BINS * PACK * C], BF16)
+        def load_frames(j):
+            frames = frames_pool.tile([P, GROUPS, FRAMES * C], BF16)
+            nc.sync.dma_start(
+                out=frames[:], in_=dram_chunk(frames_rows, j, FRAMES * C).rearrange("q (r f) -> q r f", r=GROUPS)
+            )
+            frames_of[j] = frames
+
+        def load_weights():
             nc.sync.dma_start(
                 out=w_raw[:].rearrange("q (g f) -> q g f", f=2 * C),
                 in_=Wout.rearrange("n k c -> (n k) c").rearrange("(g q e) c -> q g (e c)", q=P, e=2),
             )
-            w_grouped = const.tile([P, BINS * C * PACK], BF16, align_bytes=64)
+
+        def quantise_weights():
             nc.vector.tensor_copy(
                 out=w_grouped[:].rearrange("q (n c t) -> q n c t", n=BINS, t=PACK),
                 in_=w_raw[:].rearrange("q (n t c) -> q n c t", n=BINS, t=PACK),
             )
-            w_codes = const.tile([P, BINS * C], U32, align_bytes=64)
-            w_scales = const.tile([P, BINS * C], U8, align_bytes=64)
             nc.vector.quantize_mx(out=w_codes[:].bitcast(FP8X4), scales=w_scales[:], in_=w_grouped[:])
-            return w_codes, w_scales
 
-        def quantise_pooled(x_sb):
-            x_words = x_sb[:].bitcast(F32)
-            grouped = mx_pool.tile([P, BLOCKS * P * PACK], BF16, align_bytes=64)
-            grouped_words = grouped[:].bitcast(F32)
-            for pair in range(BLOCKS // 2):
+        def transpose(j):
+            x_words = x_of[j][:].bitcast(F32)
+            xt_of[j] = []
+            for bank in range(XT_BANKS):
                 xt = xt_pool.tile([P, 2, 2, P], F32)
-                for blk in range(2):
+                for g in range(2):
                     for u in range(2):
-                        first = ((2 * pair + blk) * 2 + u) * P
-                        nc.tensor.transpose(xt[:, blk, u, :], x_words[:, first : first + P], ident[:])
-                nc.scalar.copy(
-                    out=grouped_words[:, pair * BANK : (pair + 1) * BANK].rearrange(
-                        "q (k b u) -> q k b u", k=2, u=2
-                    ),
-                    in_=xt[:].rearrange("q k u b -> q k b u"),
-                )
-            codes = mx_pool.tile([P, BLOCKS * P], U32, align_bytes=64)
-            scales = mx_pool.tile([P, BLOCKS * P], U8, align_bytes=64)
-            nc.vector.quantize_mx(out=codes[:].bitcast(FP8X4), scales=scales[:], in_=grouped[:])
-            return codes, scales
+                        first = ((2 * bank + g) * 2 + u) * P
+                        nc.tensor.transpose(xt[:, g, u, :], x_words[:, first : first + P], ident[:])
+                xt_of[j].append(xt)
 
-        def multiply_and_leaky(i, codes, scales):
-            n = chunk_place(i)[0]
-            w_cols = slice(n * C, (n + 1) * C)
-            slope_y = work.tile([P, BLOCKS * C], F32)
-            leaky = leaky_pool.tile([P, BLOCKS * C], F32)
-            for bank in range(BLOCKS // BLOCKS_PER_Y_BANK):
+        def copy_out(j):
+            grouped = work.tile([P, GROUPS * P * PACK], BF16, align_bytes=64)
+            grouped_words = grouped[:].bitcast(F32)
+            for bank in range(XT_BANKS):
+                nc.scalar.copy(
+                    out=grouped_words[:, bank * BANK : (bank + 1) * BANK].rearrange("q (g b u) -> q g b u", g=2, u=2),
+                    in_=xt_of[j][bank][:].rearrange("q g u b -> q g b u"),
+                )
+            grouped_of[j] = grouped
+
+        def quantise(j):
+            codes = work.tile([P, GROUPS * P], U32, align_bytes=64)
+            scales = work.tile([P, GROUPS * P], U8, align_bytes=64)
+            nc.vector.quantize_mx(out=codes[:].bitcast(FP8X4), scales=scales[:], in_=grouped_of[j][:])
+            codes_of[j], scales_of[j] = codes, scales
+
+        def multiply(j):
+            w_cols = slice((j // CHUNKS_PER_BIN) * C, (j // CHUNKS_PER_BIN + 1) * C)
+            y_of[j] = []
+            for bank in range(Y_BANKS):
                 y_ps = y_pool.tile([P, BANK], F32)
-                for j in range(BLOCKS_PER_Y_BANK):
-                    b_cols = slice((bank * BLOCKS_PER_Y_BANK + j) * P, (bank * BLOCKS_PER_Y_BANK + j + 1) * P)
+                for g in range(BANK // C):
+                    b_cols = slice((bank * (BANK // C) + g) * P, (bank * (BANK // C) + g + 1) * P)
                     nc.tensor.matmul_mx(
-                        out=y_ps[:, j * C : (j + 1) * C],
-                        lhsT=codes[:, b_cols].bitcast(FP8X4),
-                        lhsT_scale=scales[:, b_cols],
+                        out=y_ps[:, g * C : (g + 1) * C],
+                        lhsT=codes_of[j][:, b_cols].bitcast(FP8X4),
+                        lhsT_scale=scales_of[j][:, b_cols],
                         rhs=w_codes[:, w_cols].bitcast(FP8X4),
                         rhs_scale=w_scales[:, w_cols],
                         start=True,
                         stop=True,
                     )
+                y_of[j].append(y_ps)
+
+        def scale_product(j):
+            slope_y = work.tile([P, GROUPS * C], F32)
+            for bank in range(Y_BANKS):
+                nc.scalar.mul(out=slope_y[:, bank * BANK : (bank + 1) * BANK], in_=y_of[j][bank][:], mul=LEAKY_SLOPE)
+            slope_of[j] = slope_y
+
+        def leaky(j):
+            leaky_y = leaky_pool.tile([P, GROUPS * C], F32)
+            for bank in range(Y_BANKS):
                 cols = slice(bank * BANK, (bank + 1) * BANK)
-                nc.scalar.mul(out=slope_y[:, cols], in_=y_ps[:], mul=LEAKY_SLOPE)
-                nc.vector.tensor_tensor(out=leaky[:, cols], in0=y_ps[:], in1=slope_y[:, cols], op=MAX)
-            return leaky
+                nc.vector.tensor_tensor(out=leaky_y[:, cols], in0=y_of[j][bank][:], in1=slope_of[j][:, cols], op=MAX)
+            leaky_of[j] = leaky_y
 
-        def add_frames_and_store(i, leaky):
-            n, r0 = chunk_place(i)
-            frames = frames_pool.tile([P, BLOCKS, FRAMES * C], BF16)
-            nc.sync.dma_start(
-                out=frames[:],
-                in_=frames_rows[n, :, r0 * FRAMES * C : (r0 + BLOCKS) * FRAMES * C].rearrange(
-                    "q (r f) -> q r f", f=FRAMES * C
-                ),
-            )
-            pair_max = work.tile([P, BLOCKS, 2 * C], BF16)
+        def pair_max(j):
+            pairs = work.tile([P, GROUPS, 2 * C], BF16)
             nc.vector.tensor_tensor(
-                out=pair_max[:], in0=frames[:, :, 0 : 2 * C], in1=frames[:, :, 2 * C : 4 * C], op=MAX
+                out=pairs[:], in0=frames_of[j][:, :, 0 : 2 * C], in1=frames_of[j][:, :, 2 * C : 4 * C], op=MAX
             )
-            frame_max = work.tile([P, BLOCKS, C], BF16)
-            nc.vector.tensor_tensor(
-                out=frame_max[:], in0=pair_max[:, :, 0:C], in1=pair_max[:, :, C : 2 * C], op=MAX
-            )
-            feat = feat_pool.tile([P, BLOCKS * C], F32)
-            nc.vector.tensor_tensor(
-                out=feat[:], in0=leaky[:], in1=frame_max[:].rearrange("q r c -> q (r c)"), op=ADD
-            )
-            nc.sync.dma_start(out=out_rows[n, :, r0 * C : (r0 + BLOCKS) * C], in_=feat[:])
+            pair_of[j] = pairs
 
-        x_first = load_pooled(0)
-        w_codes, w_scales = quantise_weights()
+        def frame_max(j):
+            fmax = work.tile([P, GROUPS, C], BF16)
+            nc.vector.tensor_tensor(out=fmax[:], in0=pair_of[j][:, :, 0:C], in1=pair_of[j][:, :, C : 2 * C], op=MAX)
+            fmax_of[j] = fmax
 
-        leaky_of = {}
-        for step in range(CHUNKS + LEAD):
-            if step < CHUNKS:
-                x_sb = x_first if step == 0 else load_pooled(step)
-                codes, scales = quantise_pooled(x_sb)
-                leaky_of[step] = multiply_and_leaky(step, codes, scales)
-            if step >= LEAD:
-                add_frames_and_store(step - LEAD, leaky_of[step - LEAD])
+        def add_and_store(j):
+            feat = feat_pool.tile([P, GROUPS * C], F32)
+            nc.vector.tensor_tensor(
+                out=feat[:], in0=leaky_of[j][:], in1=fmax_of[j][:].rearrange("q r c -> q (r c)"), op=ADD
+            )
+            nc.sync.dma_start(out=dram_chunk(out_rows, j, C), in_=feat[:])
+
+        def run(stage, j):
+            if 0 <= j < CHUNKS:
+                stage(j)
+
+        def loads_read_in_step(k):
+            run(load_frames, k - FRAME_LAG)
+            run(load_pooled, k + 2)
+
+        with tc.manual_schedule():
+            load_pooled(0)
+            load_weights()
+            load_pooled(1)
+            for k in range(AHEAD):
+                loads_read_in_step(k)
+            quantise_weights()
+            transpose(0)
+            copy_out(0)
+            transpose(1)
+            for k in range(CHUNKS + FRAME_LAG + 1):
+                loads_read_in_step(k + AHEAD)
+                run(quantise, k)
+                run(multiply, k)
+                run(copy_out, k + 1)
+                run(scale_product, k)
+                run(transpose, k + 2)
+                run(pair_max, k - FRAME_LAG)
+                run(add_and_store, k - FRAME_LAG - 1)
+                run(frame_max, k - FRAME_LAG)
+                run(leaky, k)

@@ -28,7 +28,9 @@ XT_BANKS = GROUPS * K // 2 // BANK
 Y_BANKS = GROUPS * C // BANK
 
 FRAME_LAG = 1
-AHEAD = 3
+AHEAD = 5
+GPSIMD_GROUPS = 3
+VECTOR_COLS = (GROUPS - GPSIMD_GROUPS) * C
 
 FLOPS = 2 * BINS * SAMPLES * K * C
 
@@ -50,7 +52,7 @@ def tile_gmpahead_pa_t_kernel(tc, pooled, p, Wout, out):
         frames_pool = ctx.enter_context(tc.tile_pool(name="frames", bufs=AHEAD + 2))
         work = ctx.enter_context(tc.tile_pool(name="work", bufs=2))
         leaky_pool = ctx.enter_context(tc.tile_pool(name="leaky", bufs=FRAME_LAG + 2))
-        feat_pool = ctx.enter_context(tc.tile_pool(name="feat", bufs=4))
+        feat_pool = ctx.enter_context(tc.tile_pool(name="feat", bufs=AHEAD + 2))
         xt_pool = ctx.enter_context(tc.psum_pool(name="xt", bufs=XT_BANKS))
         y_pool = ctx.enter_context(tc.psum_pool(name="y", bufs=2 * Y_BANKS))
 
@@ -62,7 +64,7 @@ def tile_gmpahead_pa_t_kernel(tc, pooled, p, Wout, out):
         w_scales = const.tile([P, BINS * C], U8, align_bytes=64)
 
         x_of, xt_of, grouped_of, codes_of, scales_of, y_of, slope_of, leaky_of = {}, {}, {}, {}, {}, {}, {}, {}
-        frames_of, pair_of, fmax_of = {}, {}, {}
+        frames_of, pair_of, fmax_of, feat_of = {}, {}, {}, {}
 
         def load_pooled(j):
             x_sb = x_pool.tile([P, GROUPS * K], BF16)
@@ -159,12 +161,24 @@ def tile_gmpahead_pa_t_kernel(tc, pooled, p, Wout, out):
             nc.vector.tensor_tensor(out=fmax[:], in0=pair_of[j][:, :, 0:C], in1=pair_of[j][:, :, C : 2 * C], op=MAX)
             fmax_of[j] = fmax
 
-        def add_and_store(j):
+        def add_on_gpsimd(j):
             feat = feat_pool.tile([P, GROUPS * C], F32)
-            nc.vector.tensor_tensor(
-                out=feat[:], in0=leaky_of[j][:], in1=fmax_of[j][:].rearrange("q r c -> q (r c)"), op=ADD
+            nc.gpsimd.tensor_tensor(
+                out=feat[:, VECTOR_COLS:],
+                in0=leaky_of[j][:, VECTOR_COLS:],
+                in1=fmax_of[j][:].rearrange("q r c -> q (r c)")[:, VECTOR_COLS:],
+                op=ADD,
             )
-            nc.sync.dma_start(out=dram_chunk(out_rows, j, C), in_=feat[:])
+            feat_of[j] = feat
+
+        def add_and_store(j):
+            nc.vector.tensor_tensor(
+                out=feat_of[j][:, :VECTOR_COLS],
+                in0=leaky_of[j][:, :VECTOR_COLS],
+                in1=fmax_of[j][:].rearrange("q r c -> q (r c)")[:, :VECTOR_COLS],
+                op=ADD,
+            )
+            nc.sync.dma_start(out=dram_chunk(out_rows, j, C), in_=feat_of[j][:])
 
         def run(stage, j):
             if 0 <= j < CHUNKS:
@@ -194,4 +208,5 @@ def tile_gmpahead_pa_t_kernel(tc, pooled, p, Wout, out):
                 run(pair_max, k - FRAME_LAG)
                 run(add_and_store, k - FRAME_LAG - 1)
                 run(frame_max, k - FRAME_LAG)
+                run(add_on_gpsimd, k - FRAME_LAG)
                 run(leaky, k)

@@ -80,8 +80,8 @@ def tile_gmpahead_pa_t_kernel(tc, pooled, p, Wout, out):
 
         def load_weights():
             nc.sync.dma_start(
-                out=w_raw[:].rearrange("q (g f) -> q g f", f=2 * C),
-                in_=Wout.rearrange("n k c -> (n k) c").rearrange("(g q e) c -> q g (e c)", q=P, e=2),
+                out=w_raw[:].rearrange("q (n f) -> q n f", n=BINS),
+                in_=Wout.rearrange("n (q t) c -> q n (t c)", t=PACK),
             )
 
         def quantise_weights():
@@ -92,14 +92,13 @@ def tile_gmpahead_pa_t_kernel(tc, pooled, p, Wout, out):
             nc.vector.quantize_mx(out=w_codes[:].bitcast(FP8X4), scales=w_scales[:], in_=w_grouped[:])
 
         def transpose(j):
-            x_words = x_of[j][:].bitcast(F32)
+            x_words = x_of[j][:].bitcast(F32).rearrange("b (g q u) -> b g u q", g=GROUPS, u=2)
             xt_of[j] = []
             for bank in range(XT_BANKS):
                 xt = xt_pool.tile([P, 2, 2, P], F32)
                 for g in range(2):
                     for u in range(2):
-                        first = ((2 * bank + g) * 2 + u) * P
-                        nc.tensor.transpose(xt[:, g, u, :], x_words[:, first : first + P], ident[:])
+                        nc.tensor.transpose(xt[:, g, u, :], x_words[:, 2 * bank + g, u, :], ident[:])
                 xt_of[j].append(xt)
 
         def copy_out(j):

@@ -10,6 +10,7 @@ U8 = mybir.dt.uint8
 FP8X4 = mybir.dt.float8_e4m3fn_x4
 MAX = mybir.AluOpType.max
 ADD = mybir.AluOpType.add
+RELU = mybir.ActivationFunctionType.Relu
 
 P = 128
 BINS = 4
@@ -26,11 +27,9 @@ CHUNKS = BINS * CHUNKS_PER_BIN
 BANK = 512
 XT_BANKS = GROUPS * K // 2 // BANK
 Y_BANKS = GROUPS * C // BANK
+BANK_GROUPS = BANK // P
 
-FRAME_LAG = 1
 AHEAD = 5
-GPSIMD_GROUPS = 3
-VECTOR_COLS = (GROUPS - GPSIMD_GROUPS) * C
 
 FLOPS = 2 * BINS * SAMPLES * K * C
 
@@ -51,10 +50,10 @@ def tile_gmpahead_pa_t_kernel(tc, pooled, p, Wout, out):
         x_pool = ctx.enter_context(tc.tile_pool(name="x", bufs=AHEAD + 2))
         frames_pool = ctx.enter_context(tc.tile_pool(name="frames", bufs=AHEAD + 2))
         work = ctx.enter_context(tc.tile_pool(name="work", bufs=2))
-        leaky_pool = ctx.enter_context(tc.tile_pool(name="leaky", bufs=FRAME_LAG + 2))
         feat_pool = ctx.enter_context(tc.tile_pool(name="feat", bufs=AHEAD + 2))
         xt_pool = ctx.enter_context(tc.psum_pool(name="xt", bufs=XT_BANKS))
-        y_pool = ctx.enter_context(tc.psum_pool(name="y", bufs=2 * Y_BANKS))
+        yt_pool = ctx.enter_context(tc.psum_pool(name="yt", bufs=Y_BANKS))
+        leaky_pool = ctx.enter_context(tc.psum_pool(name="leaky", bufs=Y_BANKS))
 
         ident = const.tile([P, P], F32)
         make_identity(nc, ident[:])
@@ -63,8 +62,8 @@ def tile_gmpahead_pa_t_kernel(tc, pooled, p, Wout, out):
         w_codes = const.tile([P, BINS * C], U32, align_bytes=64)
         w_scales = const.tile([P, BINS * C], U8, align_bytes=64)
 
-        x_of, xt_of, grouped_of, codes_of, scales_of, y_of, slope_of, leaky_of = {}, {}, {}, {}, {}, {}, {}, {}
-        frames_of, pair_of, fmax_of, feat_of = {}, {}, {}, {}
+        x_of, xt_of, grouped_of, codes_of, scales_of, yt_of, relu_of, slope_of, leaky_of = {}, {}, {}, {}, {}, {}, {}, {}, {}
+        frames_of, pair_of, fmax_of = {}, {}, {}
 
         def load_pooled(j):
             x_sb = x_pool.tile([P, GROUPS * K], BF16)
@@ -119,34 +118,46 @@ def tile_gmpahead_pa_t_kernel(tc, pooled, p, Wout, out):
 
         def multiply(j):
             w_cols = slice((j // CHUNKS_PER_BIN) * C, (j // CHUNKS_PER_BIN + 1) * C)
-            y_of[j] = []
+            yt_of[j] = []
             for bank in range(Y_BANKS):
-                y_ps = y_pool.tile([P, BANK], F32)
-                for g in range(BANK // C):
-                    b_cols = slice((bank * (BANK // C) + g) * P, (bank * (BANK // C) + g + 1) * P)
-                    nc.tensor.matmul_mx(
-                        out=y_ps[:, g * C : (g + 1) * C],
-                        lhsT=codes_of[j][:, b_cols].bitcast(FP8X4),
-                        lhsT_scale=scales_of[j][:, b_cols],
-                        rhs=w_codes[:, w_cols].bitcast(FP8X4),
-                        rhs_scale=w_scales[:, w_cols],
-                        start=True,
-                        stop=True,
-                    )
-                y_of[j].append(y_ps)
+                b_cols = slice(bank * BANK, (bank + 1) * BANK)
+                yt = yt_pool.tile([P, BANK], F32)
+                nc.tensor.matmul_mx(
+                    out=yt[:],
+                    lhsT=w_codes[:, w_cols].bitcast(FP8X4),
+                    lhsT_scale=w_scales[:, w_cols],
+                    rhs=codes_of[j][:, b_cols].bitcast(FP8X4),
+                    rhs_scale=scales_of[j][:, b_cols],
+                    start=True,
+                    stop=True,
+                )
+                yt_of[j].append(yt)
 
-        def scale_product(j):
-            slope_y = work.tile([P, GROUPS * C], F32)
-            for bank in range(Y_BANKS):
-                nc.scalar.mul(out=slope_y[:, bank * BANK : (bank + 1) * BANK], in_=y_of[j][bank][:], mul=LEAKY_SLOPE)
-            slope_of[j] = slope_y
-
-        def leaky(j):
-            leaky_y = leaky_pool.tile([P, GROUPS * C], F32)
+        def split(j):
+            relu_t = work.tile([P, GROUPS * P], F32)
+            slope_t = work.tile([P, GROUPS * P], F32)
             for bank in range(Y_BANKS):
                 cols = slice(bank * BANK, (bank + 1) * BANK)
-                nc.vector.tensor_tensor(out=leaky_y[:, cols], in0=y_of[j][bank][:], in1=slope_of[j][:, cols], op=MAX)
-            leaky_of[j] = leaky_y
+                nc.scalar.activation(out=relu_t[:, cols], in_=yt_of[j][bank][:], func=RELU, scale=1.0 - LEAKY_SLOPE)
+                nc.scalar.mul(out=slope_t[:, cols], in_=yt_of[j][bank][:], mul=LEAKY_SLOPE)
+            relu_of[j], slope_of[j] = relu_t, slope_t
+
+        def turn_back(j):
+            leaky_of[j] = []
+            for bank in range(Y_BANKS):
+                leaky_y = leaky_pool.tile([P, BANK], F32)
+                for g in range(BANK_GROUPS):
+                    b_cols = slice((bank * BANK_GROUPS + g) * P, (bank * BANK_GROUPS + g + 1) * P)
+                    c_cols = slice(g * C, (g + 1) * C)
+                    nc.tensor.matmul(
+                        out=leaky_y[:, c_cols], lhsT=relu_of[j][:, b_cols], rhs=ident[:], is_transpose=True,
+                        start=True, stop=False,
+                    )
+                    nc.tensor.matmul(
+                        out=leaky_y[:, c_cols], lhsT=slope_of[j][:, b_cols], rhs=ident[:], is_transpose=True,
+                        start=False, stop=True,
+                    )
+                leaky_of[j].append(leaky_y)
 
         def pair_max(j):
             pairs = work.tile([P, GROUPS, 2 * C], BF16)
@@ -160,32 +171,21 @@ def tile_gmpahead_pa_t_kernel(tc, pooled, p, Wout, out):
             nc.vector.tensor_tensor(out=fmax[:], in0=pair_of[j][:, :, 0:C], in1=pair_of[j][:, :, C : 2 * C], op=MAX)
             fmax_of[j] = fmax
 
-        def add_on_gpsimd(j):
-            feat = feat_pool.tile([P, GROUPS * C], F32)
-            nc.gpsimd.tensor_tensor(
-                out=feat[:, VECTOR_COLS:],
-                in0=leaky_of[j][:, VECTOR_COLS:],
-                in1=fmax_of[j][:].rearrange("q r c -> q (r c)")[:, VECTOR_COLS:],
-                op=ADD,
-            )
-            feat_of[j] = feat
-
         def add_and_store(j):
-            nc.vector.tensor_tensor(
-                out=feat_of[j][:, :VECTOR_COLS],
-                in0=leaky_of[j][:, :VECTOR_COLS],
-                in1=fmax_of[j][:].rearrange("q r c -> q (r c)")[:, :VECTOR_COLS],
-                op=ADD,
-            )
-            nc.sync.dma_start(out=dram_chunk(out_rows, j, C), in_=feat_of[j][:])
+            feat = feat_pool.tile([P, GROUPS * C], F32)
+            fmax = fmax_of[j][:].rearrange("q r c -> q (r c)")
+            for bank in range(Y_BANKS):
+                cols = slice(bank * BANK, (bank + 1) * BANK)
+                nc.vector.tensor_tensor(out=feat[:, cols], in0=leaky_of[j][bank][:], in1=fmax[:, cols], op=ADD)
+            nc.sync.dma_start(out=dram_chunk(out_rows, j, C), in_=feat[:])
 
         def run(stage, j):
             if 0 <= j < CHUNKS:
                 stage(j)
 
         def loads_read_in_step(k):
-            run(load_frames, k - FRAME_LAG)
             run(load_pooled, k + 2)
+            run(load_frames, k)
 
         with tc.manual_schedule():
             load_pooled(0)
@@ -194,18 +194,15 @@ def tile_gmpahead_pa_t_kernel(tc, pooled, p, Wout, out):
             for k in range(AHEAD):
                 loads_read_in_step(k)
             quantise_weights()
-            transpose(0)
-            copy_out(0)
-            transpose(1)
-            for k in range(CHUNKS + FRAME_LAG + 1):
-                loads_read_in_step(k + AHEAD)
-                run(quantise, k)
+            for k in range(-2, CHUNKS + 1):
+                if k >= 0:
+                    loads_read_in_step(k + AHEAD)
+                run(add_and_store, k - 1)
                 run(multiply, k)
-                run(copy_out, k + 1)
-                run(scale_product, k)
+                run(split, k)
                 run(transpose, k + 2)
-                run(pair_max, k - FRAME_LAG)
-                run(add_and_store, k - FRAME_LAG - 1)
-                run(frame_max, k - FRAME_LAG)
-                run(add_on_gpsimd, k - FRAME_LAG)
-                run(leaky, k)
+                run(copy_out, k + 2)
+                run(turn_back, k)
+                run(pair_max, k)
+                run(quantise, k + 1)
+                run(frame_max, k)

@@ -67,7 +67,11 @@ def tile_gmpahead_pa_t_kernel(tc, pooled, p, Wout, out):
 
         def load_pooled(j):
             x_sb = x_pool.tile([P, GROUPS * K], BF16)
-            nc.sync.dma_start(out=x_sb[:], in_=dram_chunk(pooled_rows, j, K))
+            parts = 2 if j == 0 else 1
+            width = GROUPS * K // parts
+            for part in range(parts):
+                cols = slice(part * width, (part + 1) * width)
+                nc.sync.dma_start(out=x_sb[:, cols], in_=dram_chunk(pooled_rows, j, K)[:, cols])
             x_of[j] = x_sb
 
         def load_frames(j):
@@ -177,7 +181,10 @@ def tile_gmpahead_pa_t_kernel(tc, pooled, p, Wout, out):
             for bank in range(Y_BANKS):
                 cols = slice(bank * BANK, (bank + 1) * BANK)
                 nc.vector.tensor_tensor(out=feat[:, cols], in0=leaky_of[j][bank][:], in1=fmax[:, cols], op=ADD)
-            nc.sync.dma_start(out=dram_chunk(out_rows, j, C), in_=feat[:])
+                if j == CHUNKS - 1:
+                    nc.sync.dma_start(out=dram_chunk(out_rows, j, C)[:, cols], in_=feat[:, cols])
+            if j < CHUNKS - 1:
+                nc.sync.dma_start(out=dram_chunk(out_rows, j, C), in_=feat[:])
 
         def run(stage, j):
             if 0 <= j < CHUNKS:
@@ -197,6 +204,9 @@ def tile_gmpahead_pa_t_kernel(tc, pooled, p, Wout, out):
             for k in range(-2, CHUNKS + 1):
                 if k >= 0:
                     loads_read_in_step(k + AHEAD)
+                draining = k + 2 >= CHUNKS
+                if draining:
+                    run(quantise, k + 1)
                 run(add_and_store, k - 1)
                 run(multiply, k)
                 run(split, k)
@@ -204,5 +214,6 @@ def tile_gmpahead_pa_t_kernel(tc, pooled, p, Wout, out):
                 run(copy_out, k + 2)
                 run(turn_back, k)
                 run(pair_max, k)
-                run(quantise, k + 1)
+                if not draining:
+                    run(quantise, k + 1)
                 run(frame_max, k)

@@ -29,7 +29,9 @@ XT_BANKS = GROUPS * K // 2 // BANK
 Y_BANKS = GROUPS * C // BANK
 BANK_GROUPS = BANK // P
 
-AHEAD = 5
+POOLED_LOADS = tuple((j, 1) for j in range(CHUNKS))
+FRAMES_LOADS = tuple((j, 1) for j in range(CHUNKS))
+LOAD_BUFS = {1: 6}
 
 FLOPS = 2 * BINS * SAMPLES * K * C
 
@@ -41,16 +43,15 @@ def tile_gmpahead_pa_t_kernel(tc, pooled, p, Wout, out):
     frames_rows = p.rearrange("n (q r) t c -> n q (r t c)", q=P)
     out_rows = out.rearrange("n (q r) c -> n q (r c)", q=P)
 
-    def dram_chunk(rows, j, width):
-        first = (j % CHUNKS_PER_BIN) * GROUPS * width
-        return rows[j // CHUNKS_PER_BIN, :, first : first + GROUPS * width]
+    def dram_chunks(rows, first, count, width):
+        start = (first % CHUNKS_PER_BIN) * GROUPS * width
+        return rows[first // CHUNKS_PER_BIN, :, start : start + count * GROUPS * width]
 
     with ExitStack() as ctx:
         const = ctx.enter_context(tc.tile_pool(name="const", bufs=1))
-        x_pool = ctx.enter_context(tc.tile_pool(name="x", bufs=AHEAD + 2))
-        frames_pool = ctx.enter_context(tc.tile_pool(name="frames", bufs=AHEAD + 2))
+        load_pool = ctx.enter_context(tc.tile_pool(name="load", bufs=1))
         work = ctx.enter_context(tc.tile_pool(name="work", bufs=2))
-        feat_pool = ctx.enter_context(tc.tile_pool(name="feat", bufs=AHEAD + 2))
+        feat_pool = ctx.enter_context(tc.tile_pool(name="feat", bufs=BINS))
         xt_pool = ctx.enter_context(tc.psum_pool(name="xt", bufs=XT_BANKS))
         yt_pool = ctx.enter_context(tc.psum_pool(name="yt", bufs=Y_BANKS))
         leaky_pool = ctx.enter_context(tc.psum_pool(name="leaky", bufs=Y_BANKS))
@@ -63,23 +64,26 @@ def tile_gmpahead_pa_t_kernel(tc, pooled, p, Wout, out):
         w_scales = const.tile([P, BINS * C], U8, align_bytes=64)
 
         x_of, xt_of, grouped_of, codes_of, scales_of, yt_of, relu_of, slope_of, leaky_of = {}, {}, {}, {}, {}, {}, {}, {}, {}
-        frames_of, pair_of, fmax_of = {}, {}, {}
+        frames_of, pair_of, fmax_of, feat_of = {}, {}, {}, {}
 
-        def load_pooled(j):
-            x_sb = x_pool.tile([P, GROUPS * K], BF16)
-            parts = 2 if j == 0 else 1
-            width = GROUPS * K // parts
+        def load_pooled(first, count):
+            x_sb = load_pool.tile([P, count * GROUPS * K], BF16, tag="x%d" % count, bufs=LOAD_BUFS[count])
+            parts = 2 if first == 0 else 1
+            width = count * GROUPS * K // parts
             for part in range(parts):
                 cols = slice(part * width, (part + 1) * width)
-                nc.sync.dma_start(out=x_sb[:, cols], in_=dram_chunk(pooled_rows, j, K)[:, cols])
-            x_of[j] = x_sb
+                nc.sync.dma_start(out=x_sb[:, cols], in_=dram_chunks(pooled_rows, first, count, K)[:, cols])
+            for i in range(count):
+                x_of[first + i] = x_sb[:, i * GROUPS * K : (i + 1) * GROUPS * K]
 
-        def load_frames(j):
-            frames = frames_pool.tile([P, GROUPS, FRAMES * C], BF16)
+        def load_frames(first, count):
+            frames = load_pool.tile([P, count * GROUPS, FRAMES * C], BF16, tag="p%d" % count, bufs=LOAD_BUFS[count])
             nc.sync.dma_start(
-                out=frames[:], in_=dram_chunk(frames_rows, j, FRAMES * C).rearrange("q (r f) -> q r f", r=GROUPS)
+                out=frames[:],
+                in_=dram_chunks(frames_rows, first, count, FRAMES * C).rearrange("q (r f) -> q r f", f=FRAMES * C),
             )
-            frames_of[j] = frames
+            for i in range(count):
+                frames_of[first + i] = frames[:, i * GROUPS : (i + 1) * GROUPS, :]
 
         def load_weights():
             nc.sync.dma_start(
@@ -94,15 +98,14 @@ def tile_gmpahead_pa_t_kernel(tc, pooled, p, Wout, out):
             )
             nc.vector.quantize_mx(out=w_codes[:].bitcast(FP8X4), scales=w_scales[:], in_=w_grouped[:])
 
-        def transpose(j):
-            x_words = x_of[j][:].bitcast(F32).rearrange("b (g q u) -> b g u q", g=GROUPS, u=2)
-            xt_of[j] = []
-            for bank in range(XT_BANKS):
+        def transpose(j, banks):
+            x_words = x_of[j].bitcast(F32).rearrange("b (g q u) -> b g u q", g=GROUPS, u=2)
+            for bank in banks:
                 xt = xt_pool.tile([P, 2, 2, P], F32)
                 for g in range(2):
                     for u in range(2):
                         nc.tensor.transpose(xt[:, g, u, :], x_words[:, 2 * bank + g, u, :], ident[:])
-                xt_of[j].append(xt)
+                xt_of[j, bank] = xt
 
         def copy_out(j):
             grouped = work.tile([P, GROUPS * P * PACK], BF16, align_bytes=64)
@@ -110,7 +113,7 @@ def tile_gmpahead_pa_t_kernel(tc, pooled, p, Wout, out):
             for bank in range(XT_BANKS):
                 nc.scalar.copy(
                     out=grouped_words[:, bank * BANK : (bank + 1) * BANK].rearrange("q (g b u) -> q g b u", g=2, u=2),
-                    in_=xt_of[j][bank][:].rearrange("q g u b -> q g b u"),
+                    in_=xt_of[j, bank][:].rearrange("q g u b -> q g b u"),
                 )
             grouped_of[j] = grouped
 
@@ -146,22 +149,20 @@ def tile_gmpahead_pa_t_kernel(tc, pooled, p, Wout, out):
                 nc.scalar.mul(out=slope_t[:, cols], in_=yt_of[j][bank][:], mul=LEAKY_SLOPE)
             relu_of[j], slope_of[j] = relu_t, slope_t
 
-        def turn_back(j):
-            leaky_of[j] = []
-            for bank in range(Y_BANKS):
-                leaky_y = leaky_pool.tile([P, BANK], F32)
-                for g in range(BANK_GROUPS):
-                    b_cols = slice((bank * BANK_GROUPS + g) * P, (bank * BANK_GROUPS + g + 1) * P)
-                    c_cols = slice(g * C, (g + 1) * C)
-                    nc.tensor.matmul(
-                        out=leaky_y[:, c_cols], lhsT=relu_of[j][:, b_cols], rhs=ident[:], is_transpose=True,
-                        start=True, stop=False,
-                    )
-                    nc.tensor.matmul(
-                        out=leaky_y[:, c_cols], lhsT=slope_of[j][:, b_cols], rhs=ident[:], is_transpose=True,
-                        start=False, stop=True,
-                    )
-                leaky_of[j].append(leaky_y)
+        def turn_back(j, bank):
+            leaky_y = leaky_pool.tile([P, BANK], F32)
+            for g in range(BANK_GROUPS):
+                b_cols = slice((bank * BANK_GROUPS + g) * P, (bank * BANK_GROUPS + g + 1) * P)
+                c_cols = slice(g * C, (g + 1) * C)
+                nc.tensor.matmul(
+                    out=leaky_y[:, c_cols], lhsT=relu_of[j][:, b_cols], rhs=ident[:], is_transpose=True,
+                    start=True, stop=False,
+                )
+                nc.tensor.matmul(
+                    out=leaky_y[:, c_cols], lhsT=slope_of[j][:, b_cols], rhs=ident[:], is_transpose=True,
+                    start=False, stop=True,
+                )
+            leaky_of[j, bank] = leaky_y
 
         def pair_max(j):
             pairs = work.tile([P, GROUPS, 2 * C], BF16)
@@ -175,45 +176,67 @@ def tile_gmpahead_pa_t_kernel(tc, pooled, p, Wout, out):
             nc.vector.tensor_tensor(out=fmax[:], in0=pair_of[j][:, :, 0:C], in1=pair_of[j][:, :, C : 2 * C], op=MAX)
             fmax_of[j] = fmax
 
-        def add_and_store(j):
-            feat = feat_pool.tile([P, GROUPS * C], F32)
+        def add(j):
+            if j % CHUNKS_PER_BIN == 0:
+                feat_of[j // CHUNKS_PER_BIN] = feat_pool.tile([P, CHUNKS_PER_BIN * GROUPS * C], F32, name="feat")
+            feat = feat_of[j // CHUNKS_PER_BIN]
+            first = (j % CHUNKS_PER_BIN) * GROUPS * C
             fmax = fmax_of[j][:].rearrange("q r c -> q (r c)")
             for bank in range(Y_BANKS):
                 cols = slice(bank * BANK, (bank + 1) * BANK)
-                nc.vector.tensor_tensor(out=feat[:, cols], in0=leaky_of[j][bank][:], in1=fmax[:, cols], op=ADD)
-                if j == CHUNKS - 1:
-                    nc.sync.dma_start(out=dram_chunk(out_rows, j, C)[:, cols], in_=feat[:, cols])
-            if j < CHUNKS - 1:
-                nc.sync.dma_start(out=dram_chunk(out_rows, j, C), in_=feat[:])
+                out_cols = slice(first + bank * BANK, first + (bank + 1) * BANK)
+                nc.vector.tensor_tensor(out=feat[:, out_cols], in0=leaky_of[j, bank][:], in1=fmax[:, cols], op=ADD)
 
-        def run(stage, j):
+        def store(j):
+            last_bin = j // CHUNKS_PER_BIN == BINS - 1
+            if not last_bin and (j + 1) % CHUNKS_PER_BIN:
+                return
+            chunks = 1 if last_bin else CHUNKS_PER_BIN
+            parts = Y_BANKS if j == CHUNKS - 1 else 1
+            width = chunks * GROUPS * C // parts
+            first = ((j + 1) % CHUNKS_PER_BIN - chunks) % CHUNKS_PER_BIN * GROUPS * C
+            for part in range(parts):
+                cols = slice(first + part * width, first + (part + 1) * width)
+                nc.sync.dma_start(out=out_rows[j // CHUNKS_PER_BIN, :, cols], in_=feat_of[j // CHUNKS_PER_BIN][:, cols])
+
+        def run(stage, j, *part):
             if 0 <= j < CHUNKS:
-                stage(j)
+                stage(j, *part)
 
-        def loads_read_in_step(k):
-            run(load_pooled, k + 2)
-            run(load_frames, k)
+        loads = [(first - 2, load_pooled, first, count) for first, count in POOLED_LOADS]
+        loads += [(first, load_frames, first, count) for first, count in FRAMES_LOADS]
+        loads = sorted(loads, key=lambda load: load[0])
+
+        last_read, asked_for, stored = {}, [], []
+
+        def ask(k):
+            for step, load, first, count in loads[len(asked_for) :]:
+                last_reads = last_read.setdefault((load, count), [])
+                if len(last_reads) >= LOAD_BUFS[count] and last_reads[-LOAD_BUFS[count]] > k:
+                    return
+                load(first, count)
+                if first == 1 and load is load_pooled:
+                    load_weights()
+                last_reads.append(step + count - 1)
+                asked_for.append(first)
 
         with tc.manual_schedule():
-            load_pooled(0)
-            load_weights()
-            load_pooled(1)
-            for k in range(AHEAD):
-                loads_read_in_step(k)
-            quantise_weights()
+            ask(-3)
             for k in range(-2, CHUNKS + 1):
-                if k >= 0:
-                    loads_read_in_step(k + AHEAD)
-                draining = k + 2 >= CHUNKS
-                if draining:
-                    run(quantise, k + 1)
-                run(add_and_store, k - 1)
+                run(add, k - 1)
                 run(multiply, k)
                 run(split, k)
-                run(transpose, k + 2)
+                for bank in range(Y_BANKS):
+                    run(transpose, k + 2, range(bank * XT_BANKS // Y_BANKS, (bank + 1) * XT_BANKS // Y_BANKS))
+                    run(turn_back, k, bank)
                 run(copy_out, k + 2)
-                run(turn_back, k)
                 run(pair_max, k)
-                if not draining:
-                    run(quantise, k + 1)
+                run(quantise, k + 1)
+                if k == -1:
+                    quantise_weights()
                 run(frame_max, k)
+                ask(k)
+                if len(asked_for) == len(loads):
+                    for j in range(len(stored), k):
+                        store(j)
+                        stored.append(j)

@@ -86,10 +86,11 @@ def tile_gmpahead_pa_t_kernel(tc, pooled, p, Wout, out):
                 frames_of[first + i] = frames[:, i * GROUPS : (i + 1) * GROUPS, :]
 
         def load_weights():
-            nc.sync.dma_start(
-                out=w_raw[:].rearrange("q (n f) -> q n f", n=BINS),
-                in_=Wout.rearrange("n (q t) c -> q n (t c)", t=PACK),
-            )
+            for u in range(2):
+                nc.sync.dma_start(
+                    out=w_raw[:].rearrange("q (n u f) -> q u n f", n=BINS, u=2)[:, u],
+                    in_=Wout.rearrange("n (u q e) c -> u q n (e c)", u=2, q=P)[u],
+                )
 
         def quantise_weights():
             nc.vector.tensor_copy(
@@ -99,7 +100,7 @@ def tile_gmpahead_pa_t_kernel(tc, pooled, p, Wout, out):
             nc.vector.quantize_mx(out=w_codes[:].bitcast(FP8X4), scales=w_scales[:], in_=w_grouped[:])
 
         def transpose(j, banks):
-            x_words = x_of[j].bitcast(F32).rearrange("b (g q u) -> b g u q", g=GROUPS, u=2)
+            x_words = x_of[j].bitcast(F32).rearrange("b (g u q) -> b g u q", g=GROUPS, u=2)
             for bank in banks:
                 xt = xt_pool.tile([P, 2, 2, P], F32)
                 for g in range(2):

@@ -29,9 +29,9 @@ XT_BANKS = GROUPS * K // 2 // BANK
 Y_BANKS = GROUPS * C // BANK
 BANK_GROUPS = BANK // P
 
-POOLED_LOADS = tuple((j, 1) for j in range(CHUNKS))
-FRAMES_LOADS = tuple((j, 1) for j in range(CHUNKS))
-LOAD_BUFS = {1: 6}
+POOLED_LOADS = ((0, 1), (1, 1), (2, 1), (3, 1), (4, 2), (6, 1), (7, 2), (9, 1), (10, 2))
+FRAMES_LOADS = ((0, 1), (1, 1), (2, 1), (3, 1), (4, 2), (6, 1), (7, 2), (9, 2), (11, 1))
+LOAD_BUFS = {1: 3, 2: 2}
 
 FLOPS = 2 * BINS * SAMPLES * K * C
 
@@ -189,15 +189,15 @@ def tile_gmpahead_pa_t_kernel(tc, pooled, p, Wout, out):
                 nc.vector.tensor_tensor(out=feat[:, out_cols], in0=leaky_of[j, bank][:], in1=fmax[:, cols], op=ADD)
 
         def store(j):
-            last_bin = j // CHUNKS_PER_BIN == BINS - 1
-            if not last_bin and (j + 1) % CHUNKS_PER_BIN:
+            bin_end = (j + 1) % CHUNKS_PER_BIN == 0
+            if not bin_end and j != CHUNKS - 2:
                 return
-            chunks = 1 if last_bin else CHUNKS_PER_BIN
+            chunks = 1 if j == CHUNKS - 1 else CHUNKS_PER_BIN if bin_end else CHUNKS_PER_BIN - 1
             parts = Y_BANKS if j == CHUNKS - 1 else 1
             width = chunks * GROUPS * C // parts
-            first = ((j + 1) % CHUNKS_PER_BIN - chunks) % CHUNKS_PER_BIN * GROUPS * C
-            for part in range(parts):
-                cols = slice(first + part * width, first + (part + 1) * width)
+            end = (j % CHUNKS_PER_BIN + 1) * GROUPS * C
+            for first in range(end - parts * width, end, width):
+                cols = slice(first, first + width)
                 nc.sync.dma_start(out=out_rows[j // CHUNKS_PER_BIN, :, cols], in_=feat_of[j // CHUNKS_PER_BIN][:, cols])
 
         def run(stage, j, *part):

from contextlib import ExitStack

import concourse.mybir as mybir
from concourse.masks import make_identity

F32 = mybir.dt.float32
BF16 = mybir.dt.bfloat16
U32 = mybir.dt.uint32
U8 = mybir.dt.uint8
FP8X4 = mybir.dt.float8_e4m3fn_x4
MAX = mybir.AluOpType.max
ADD = mybir.AluOpType.add
RELU = mybir.ActivationFunctionType.Relu

P = 128
BINS = 4
SAMPLES = 3072
FRAMES = 4
C = 128
K = 512
PACK = 4
LEAKY_SLOPE = 0.01

GROUPS = 8
CHUNKS_PER_BIN = SAMPLES // (P * GROUPS)
CHUNKS = BINS * CHUNKS_PER_BIN
BANK = 512
XT_BANKS = GROUPS * K // 2 // BANK
Y_BANKS = GROUPS * C // BANK
BANK_GROUPS = BANK // P

POOLED_LOADS = ((0, 1), (1, 1), (2, 1), (3, 1), (4, 2), (6, 1), (7, 2), (9, 1), (10, 2))
FRAMES_LOADS = ((0, 1), (1, 1), (2, 1), (3, 1), (4, 2), (6, 1), (7, 2), (9, 2), (11, 1))
LOAD_BUFS = {1: 3, 2: 2}

FLOPS = 2 * BINS * SAMPLES * K * C


def tile_gmpahead_pa_t_kernel(tc, pooled, p, Wout, out):
    nc = tc.nc

    pooled_rows = pooled.rearrange("n (q r) k -> n q (r k)", q=P)
    frames_rows = p.rearrange("n (q r) t c -> n q (r t c)", q=P)
    out_rows = out.rearrange("n (q r) c -> n q (r c)", q=P)

    def dram_chunks(rows, first, count, width):
        start = (first % CHUNKS_PER_BIN) * GROUPS * width
        return rows[first // CHUNKS_PER_BIN, :, start : start + count * GROUPS * width]

    with ExitStack() as ctx:
        const = ctx.enter_context(tc.tile_pool(name="const", bufs=1))
        load_pool = ctx.enter_context(tc.tile_pool(name="load", bufs=1))
        work = ctx.enter_context(tc.tile_pool(name="work", bufs=2))
        feat_pool = ctx.enter_context(tc.tile_pool(name="feat", bufs=BINS))
        xt_pool = ctx.enter_context(tc.psum_pool(name="xt", bufs=XT_BANKS))
        yt_pool = ctx.enter_context(tc.psum_pool(name="yt", bufs=Y_BANKS))
        leaky_pool = ctx.enter_context(tc.psum_pool(name="leaky", bufs=Y_BANKS))

        ident = const.tile([P, P], F32)
        make_identity(nc, ident[:])
        w_raw = const.tile([P, BINS * PACK * C], BF16)
        w_grouped = const.tile([P, BINS * C * PACK], BF16, align_bytes=64)
        w_codes = const.tile([P, BINS * C], U32, align_bytes=64)
        w_scales = const.tile([P, BINS * C], U8, align_bytes=64)

        x_of, xt_of, grouped_of, codes_of, scales_of, yt_of, relu_of, slope_of, leaky_of = {}, {}, {}, {}, {}, {}, {}, {}, {}
        frames_of, pair_of, fmax_of, feat_of = {}, {}, {}, {}

        def load_pooled(first, count):
            x_sb = load_pool.tile([P, count * GROUPS * K], BF16, tag="x%d" % count, bufs=LOAD_BUFS[count])
            parts = 2 if first == 0 else 1
            width = count * GROUPS * K // parts
            for part in range(parts):
                cols = slice(part * width, (part + 1) * width)
                nc.sync.dma_start(out=x_sb[:, cols], in_=dram_chunks(pooled_rows, first, count, K)[:, cols])
            for i in range(count):
                x_of[first + i] = x_sb[:, i * GROUPS * K : (i + 1) * GROUPS * K]

        def load_frames(first, count):
            frames = load_pool.tile([P, count * GROUPS, FRAMES * C], BF16, tag="p%d" % count, bufs=LOAD_BUFS[count])
            nc.sync.dma_start(
                out=frames[:],
                in_=dram_chunks(frames_rows, first, count, FRAMES * C).rearrange("q (r f) -> q r f", f=FRAMES * C),
            )
            for i in range(count):
                frames_of[first + i] = frames[:, i * GROUPS : (i + 1) * GROUPS, :]

        def load_weights():
            for u in range(2):
                nc.sync.dma_start(
                    out=w_raw[:].rearrange("q (n u f) -> q u n f", n=BINS, u=2)[:, u],
                    in_=Wout.rearrange("n (u q e) c -> u q n (e c)", u=2, q=P)[u],
                )

        def quantise_weights():
            nc.vector.tensor_copy(
                out=w_grouped[:].rearrange("q (n c t) -> q n c t", n=BINS, t=PACK),
                in_=w_raw[:].rearrange("q (n t c) -> q n c t", n=BINS, t=PACK),
            )
            nc.vector.quantize_mx(out=w_codes[:].bitcast(FP8X4), scales=w_scales[:], in_=w_grouped[:])

        def transpose(j, banks):
            x_words = x_of[j].bitcast(F32).rearrange("b (g u q) -> b g u q", g=GROUPS, u=2)
            for bank in banks:
                xt = xt_pool.tile([P, 2, 2, P], F32)
                for g in range(2):
                    for u in range(2):
                        nc.tensor.transpose(xt[:, g, u, :], x_words[:, 2 * bank + g, u, :], ident[:])
                xt_of[j, bank] = xt

        def copy_out(j):
            grouped = work.tile([P, GROUPS * P * PACK], BF16, align_bytes=64)
            grouped_words = grouped[:].bitcast(F32)
            for bank in range(XT_BANKS):
                nc.scalar.copy(
                    out=grouped_words[:, bank * BANK : (bank + 1) * BANK].rearrange("q (g b u) -> q g b u", g=2, u=2),
                    in_=xt_of[j, bank][:].rearrange("q g u b -> q g b u"),
                )
            grouped_of[j] = grouped

        def quantise(j):
            codes = work.tile([P, GROUPS * P], U32, align_bytes=64)
            scales = work.tile([P, GROUPS * P], U8, align_bytes=64)
            nc.vector.quantize_mx(out=codes[:].bitcast(FP8X4), scales=scales[:], in_=grouped_of[j][:])
            codes_of[j], scales_of[j] = codes, scales

        def multiply(j):
            w_cols = slice((j // CHUNKS_PER_BIN) * C, (j // CHUNKS_PER_BIN + 1) * C)
            yt_of[j] = []
            for bank in range(Y_BANKS):
                b_cols = slice(bank * BANK, (bank + 1) * BANK)
                yt = yt_pool.tile([P, BANK], F32)
                nc.tensor.matmul_mx(
                    out=yt[:],
                    lhsT=w_codes[:, w_cols].bitcast(FP8X4),
                    lhsT_scale=w_scales[:, w_cols],
                    rhs=codes_of[j][:, b_cols].bitcast(FP8X4),
                    rhs_scale=scales_of[j][:, b_cols],
                    start=True,
                    stop=True,
                )
                yt_of[j].append(yt)

        def split(j):
            relu_t = work.tile([P, GROUPS * P], F32)
            slope_t = work.tile([P, GROUPS * P], F32)
            for bank in range(Y_BANKS):
                cols = slice(bank * BANK, (bank + 1) * BANK)
                nc.scalar.activation(out=relu_t[:, cols], in_=yt_of[j][bank][:], func=RELU, scale=1.0 - LEAKY_SLOPE)
                nc.scalar.mul(out=slope_t[:, cols], in_=yt_of[j][bank][:], mul=LEAKY_SLOPE)
            relu_of[j], slope_of[j] = relu_t, slope_t

        def turn_back(j, bank):
            leaky_y = leaky_pool.tile([P, BANK], F32)
            for g in range(BANK_GROUPS):
                b_cols = slice((bank * BANK_GROUPS + g) * P, (bank * BANK_GROUPS + g + 1) * P)
                c_cols = slice(g * C, (g + 1) * C)
                nc.tensor.matmul(
                    out=leaky_y[:, c_cols], lhsT=relu_of[j][:, b_cols], rhs=ident[:], is_transpose=True,
                    start=True, stop=False,
                )
                nc.tensor.matmul(
                    out=leaky_y[:, c_cols], lhsT=slope_of[j][:, b_cols], rhs=ident[:], is_transpose=True,
                    start=False, stop=True,
                )
            leaky_of[j, bank] = leaky_y

        def pair_max(j):
            pairs = work.tile([P, GROUPS, 2 * C], BF16)
            nc.vector.tensor_tensor(
                out=pairs[:], in0=frames_of[j][:, :, 0 : 2 * C], in1=frames_of[j][:, :, 2 * C : 4 * C], op=MAX
            )
            pair_of[j] = pairs

        def frame_max(j):
            fmax = work.tile([P, GROUPS, C], BF16)
            nc.vector.tensor_tensor(out=fmax[:], in0=pair_of[j][:, :, 0:C], in1=pair_of[j][:, :, C : 2 * C], op=MAX)
            fmax_of[j] = fmax

        def add(j):
            if j % CHUNKS_PER_BIN == 0:
                feat_of[j // CHUNKS_PER_BIN] = feat_pool.tile([P, CHUNKS_PER_BIN * GROUPS * C], F32, name="feat")
            feat = feat_of[j // CHUNKS_PER_BIN]
            first = (j % CHUNKS_PER_BIN) * GROUPS * C
            fmax = fmax_of[j][:].rearrange("q r c -> q (r c)")
            for bank in range(Y_BANKS):
                cols = slice(bank * BANK, (bank + 1) * BANK)
                out_cols = slice(first + bank * BANK, first + (bank + 1) * BANK)
                nc.vector.tensor_tensor(out=feat[:, out_cols], in0=leaky_of[j, bank][:], in1=fmax[:, cols], op=ADD)

        def store(j):
            bin_end = (j + 1) % CHUNKS_PER_BIN == 0
            if not bin_end and j != CHUNKS - 2:
                return
            chunks = 1 if j == CHUNKS - 1 else CHUNKS_PER_BIN if bin_end else CHUNKS_PER_BIN - 1
            parts = Y_BANKS if j == CHUNKS - 1 else 1
            width = chunks * GROUPS * C // parts
            end = (j % CHUNKS_PER_BIN + 1) * GROUPS * C
            for first in range(end - parts * width, end, width):
                cols = slice(first, first + width)
                nc.sync.dma_start(out=out_rows[j // CHUNKS_PER_BIN, :, cols], in_=feat_of[j // CHUNKS_PER_BIN][:, cols])

        def run(stage, j, *part):
            if 0 <= j < CHUNKS:
                stage(j, *part)

        loads = [(first - 2, load_pooled, first, count) for first, count in POOLED_LOADS]
        loads += [(first, load_frames, first, count) for first, count in FRAMES_LOADS]
        loads = sorted(loads, key=lambda load: load[0])

        last_read, asked_for, stored = {}, [], []

        def ask(k):
            for step, load, first, count in loads[len(asked_for) :]:
                last_reads = last_read.setdefault((load, count), [])
                if len(last_reads) >= LOAD_BUFS[count] and last_reads[-LOAD_BUFS[count]] > k:
                    return
                load(first, count)
                if first == 1 and load is load_pooled:
                    load_weights()
                last_reads.append(step + count - 1)
                asked_for.append(first)

        with tc.manual_schedule():
            ask(-3)
            for k in range(-2, CHUNKS + 1):
                run(add, k - 1)
                run(multiply, k)
                run(split, k)
                for bank in range(Y_BANKS):
                    run(transpose, k + 2, range(bank * XT_BANKS // Y_BANKS, (bank + 1) * XT_BANKS // Y_BANKS))
                    run(turn_back, k, bank)
                run(copy_out, k + 2)
                run(pair_max, k)
                run(quantise, k + 1)
                if k == -1:
                    quantise_weights()
                run(frame_max, k)
                ask(k)
                if len(asked_for) == len(loads):
                    for j in range(len(stored), k):
                        store(j)
                        stored.append(j)
